import numpy as np
import ml_dtypes


def mxq(x, axis, fmt="e4m3"):
    dtype, down = {"e4m3": (ml_dtypes.float8_e4m3fn, 7), "e5m2": (ml_dtypes.float8_e5m2, 14)}[fmt]
    v = np.moveaxis(np.asarray(x, np.float32).astype(ml_dtypes.bfloat16).astype(np.float64), axis, -1)
    blocks = v.reshape(v.shape[:-1] + (-1, 32))
    amax = np.abs(blocks).max(-1, keepdims=True)
    byte = np.maximum(np.where(amax > 0, np.frexp(amax)[1] - 1 + 127, 0) - down, 1)
    scale = np.exp2(byte - 127.0)
    codes = (blocks / scale).astype(np.float32).astype(dtype).astype(np.float64)
    return np.moveaxis((codes * scale).reshape(v.shape), -1, axis)


WIDE = False


def mx_kscale(k):
    if not WIDE:
        return np.ones(k)
    levels = np.array([10, -10, 5, -5, 0])
    if k % 512:
        return np.exp2(np.random.permutation(np.resize(levels, k // 32))).repeat(32)
    a = np.empty((k // 512, 16))
    for p in range(k // 512):
        a[p, :8] = np.random.permutation(np.resize(levels, 8))
        for g in range(8):
            far = levels[np.abs(levels - a[p, g]) >= 10]
            a[p, g + 8] = far[np.random.randint(len(far))]
    return np.exp2(a.ravel()).repeat(32)


BF16 = ml_dtypes.bfloat16


def bf(x):
    return np.asarray(x, np.float32).astype(BF16)


def f64(x):
    return np.asarray(x).astype(np.float64)


B, S, D, H, HD = 2, 512, 1024, 8, 128
W = H * HD
THETA = 10000.0


def rotary(t, cos, sin):
    tr = t.reshape(t.shape[:-1] + (-1, 2))
    te, to = tr[..., 0], tr[..., 1]
    oe = te * cos - to * sin
    oo = te * sin + to * cos
    return np.stack([oe, oo], axis=-1).reshape(t.shape)


def heads(y):
    return y.reshape(B, S, H, HD).transpose(0, 2, 1, 3)


def setup_inputs():
    s = mx_kscale(D)
    inv_freq = 1.0 / THETA ** (np.arange(0, HD, 2) / HD)
    ang = np.arange(S)[:, None] * inv_freq[None, :]
    return {"x": bf(np.random.standard_normal((B, S, D)) * s),
            "wq": bf(np.random.standard_normal((H, HD, D)) / np.sqrt(D) / s),
            "wk": bf(np.random.standard_normal((H, HD, D)) / np.sqrt(D) / s),
            "wv": bf(np.random.standard_normal((H, HD, D)) / np.sqrt(D) / s),
            "freqs_cos": bf(np.cos(ang)), "freqs_sin": bf(np.sin(ang))}


def reference(x, wq, wk, wv, freqs_cos, freqs_sin):
    xq = mxq(f64(x), 2, "e4m3")
    q = xq @ mxq(f64(wq).reshape(W, D), 1, "e4m3").T
    k = xq @ mxq(f64(wk).reshape(W, D), 1, "e4m3").T
    v = xq @ mxq(f64(wv).reshape(W, D), 1, "e4m3").T
    cos, sin = f64(freqs_cos), f64(freqs_sin)
    return rotary(heads(q), cos, sin), rotary(heads(k), cos, sin), heads(v)

@@ -1,0 +1,244 @@
+from contextlib import ExitStack
+
+import concourse.mybir as mybir
+from concourse.masks import make_identity
+
+F32 = mybir.dt.float32
+BF16 = mybir.dt.bfloat16
+U32 = mybir.dt.uint32
+U8 = mybir.dt.uint8
+FP8X4 = mybir.dt.float8_e4m3fn_x4
+MULT = mybir.AluOpType.mult
+ADD = mybir.AluOpType.add
+
+B, S, D, H, HD = 2, 512, 1024, 8, 128
+P = 128
+PACK = 4
+K_PASS = P * PACK
+PASSES = D // K_PASS
+U = 2
+TILES = 4
+ROWS = TILES * P
+PAIRS = HD // 2
+Q, K, V = 0, 1, 2
+
+FLOPS = 2 * B * S * D * 3 * H * HD
+
+
+def tile_attention_pa_kernel(tc, x, wq, wk, wv, freqs_cos, freqs_sin, out_0, out_1, out_2):
+    nc = tc.nc
+    weights = [wq, wk, wv]
+    outs = [out_0, out_1, out_2]
+
+    with ExitStack() as ctx:
+        ctx.enter_context(tc.manual_schedule())
+        const = ctx.enter_context(tc.tile_pool(name="const", bufs=1))
+        raw_pool = ctx.enter_context(tc.tile_pool(name="raw", bufs=8))
+        grouped_pool = ctx.enter_context(tc.tile_pool(name="grouped", bufs=3))
+        operand_pool = ctx.enter_context(tc.tile_pool(name="operand", bufs=8))
+        product_pool = ctx.enter_context(tc.tile_pool(name="product", bufs=3))
+        staged_pool = ctx.enter_context(tc.tile_pool(name="staged", bufs=4))
+        flipped_psum = ctx.enter_context(tc.psum_pool(name="flipped", bufs=3))
+        rotated_psum = ctx.enter_context(tc.psum_pool(name="rotated", bufs=3))
+        plain_psum = ctx.enter_context(tc.psum_pool(name="plain", bufs=2))
+
+        tables = const.tile([P, 3, TILES * PAIRS], BF16)
+        nc.scalar.dma_start(out=tables[:, 1, :], in_=freqs_cos.rearrange("(p i) n -> p (i n)", i=TILES))
+        nc.scalar.dma_start(out=tables[:, 2, :], in_=freqs_sin.rearrange("(p i) n -> p (i n)", i=TILES))
+
+        raws = {}
+
+        def new_raw(key):
+            raw = raw_pool.tile([P, TILES, D], BF16)
+            raws[key] = raw
+
+        def load_x(b, first, count):
+            rows = x[b].rearrange("(p i) d -> p i d", i=TILES)
+            nc.sync.dma_start(out=raws[("x", b)][:, first : first + count, :], in_=rows[:, first : first + count, :])
+
+        def load_w(projection, group, first, count):
+            heads = weights[projection][group * TILES : (group + 1) * TILES]
+            rows = heads.rearrange("(a h) (n e) d -> a (h n) e d", a=2, e=2)
+            for a in range(first, first + count):
+                nc.sync.dma_start(out=raws[(projection, group)][:, 2 * a : 2 * a + 2, :], in_=rows[a])
+
+        new_raw(("x", 0))
+        new_raw((Q, 0))
+        load_x(0, 0, 1)
+        load_w(Q, 0, 0, 2)
+        load_x(0, 1, 3)
+        for key in [(K, 0), ("x", 1), (V, 0), (Q, 1), (K, 1), (V, 1)]:
+            new_raw(key)
+            if key[0] == "x":
+                load_x(1, 0, 4)
+            else:
+                load_w(key[0], key[1], 0, 2)
+
+        identity = const.tile([P, P], F32)
+        make_identity(nc, identity[:])
+
+        factors = const.tile([P, TILES, 2, 2, HD], BF16)
+        nc.vector.tensor_scalar_mul(out=tables[:, 0, :], in0=tables[:, 2, :], scalar1=-1.0)
+        for e in range(2):
+            for h in range(2):
+                nc.vector.tensor_copy(
+                    out=factors[:, :, e, h, :].rearrange("p i (n d) -> p i n d", d=2),
+                    in_=tables[:, 1 - e : 3 - e, :].rearrange("p d (i n) -> p i n d", i=TILES),
+                )
+
+        grouped = {}
+        codes = {}
+        scales = {}
+
+        def words_of(key):
+            return raws[key][:].rearrange("p t d -> p (t d)").bitcast(F32)
+
+        def transpose4(key, picks):
+            words = words_of(key)
+            flipped = flipped_psum.tile([P, 2, U, P], F32)
+            for j, (t, g) in enumerate(picks):
+                first = (t * PASSES + g) * 2 * P
+                for u in range(U):
+                    nc.tensor.transpose(flipped[:, j, u, :], words[:, first + u : first + 2 * P : 2], identity[:])
+            return flipped
+
+        def new_grouped(key):
+            g = grouped_pool.tile([P, 2 * ROWS * PACK], BF16, align_bytes=64)
+            grouped[key] = g
+            c = operand_pool.tile([P, 2 * ROWS], U32, align_bytes=64)
+            s = operand_pool.tile([P, 2 * ROWS], U8, align_bytes=64)
+            codes[key] = c
+            scales[key] = s
+
+        def transpose_x(b, t):
+            key = ("x", b)
+            flipped = transpose4(key, [(t, 0), (t, 1)])
+            words = grouped[key][:].bitcast(F32)
+            nc.scalar.copy(
+                out=words[:, t * 512 : (t + 1) * 512].rearrange("p (g r u) -> p g r u", g=2, u=U),
+                in_=flipped[:].rearrange("p g u r -> p g r u"),
+            )
+
+        def transpose_w(key, a):
+            words = grouped[key][:].bitcast(F32)
+            for g in range(PASSES):
+                flipped = transpose4(key, [(2 * a, g), (2 * a + 1, g)])
+                out = words[:, (2 * g + a) * 512 : (2 * g + a + 1) * 512]
+                if key[0] == V:
+                    nc.scalar.copy(
+                        out=out.rearrange("p (r e u) -> p r e u", e=2, u=U),
+                        in_=flipped[:].rearrange("p e u r -> p r e u"),
+                    )
+                else:
+                    nc.scalar.copy(
+                        out=out.rearrange("p (e r u) -> p e r u", e=2, u=U),
+                        in_=flipped[:].rearrange("p e u r -> p e r u"),
+                    )
+
+        def quantise(key, first, count):
+            nc.vector.quantize_mx(
+                out=codes[key][:, first : first + count].bitcast(FP8X4),
+                scales=scales[key][:, first : first + count],
+                in_=grouped[key][:, first * PACK : (first + count) * PACK],
+            )
+
+        def project(acc, b, i, key):
+            xk = ("x", b)
+            for g in range(PASSES):
+                tokens = slice((i * PASSES + g) * P, (i * PASSES + g + 1) * P)
+                rows = slice(g * ROWS, (g + 1) * ROWS)
+                nc.tensor.matmul_mx(
+                    out=acc[:],
+                    lhsT=codes[xk][:, tokens].bitcast(FP8X4),
+                    lhsT_scale=scales[xk][:, tokens],
+                    rhs=codes[key][:, rows].bitcast(FP8X4),
+                    rhs_scale=scales[key][:, rows],
+                    start=(g == 0),
+                    stop=(g == PASSES - 1),
+                )
+
+        def multiply(acc, i, products, slot):
+            shape = [P, 2, 2 * P, 2]
+            nc.vector.tensor_tensor(
+                out=products[:, :, slot, :, :].rearrange("p e a (q d) -> p a e q d", d=2),
+                in0=acc[:].rearrange("p (a e q) -> p a e q", a=2, e=2).unsqueeze(4).to_broadcast([P, 2, 2, P, 2]),
+                in1=factors[:, i].rearrange("p e h (n d) -> p e (h n) d", d=2).unsqueeze(1).to_broadcast([P, 2, 2, P, 2]),
+                op=MULT,
+            )
+
+        def add(products, staged, first):
+            nc.gpsimd.tensor_tensor(
+                out=staged[:, :, first : first + 2, :].rearrange("p h i j -> p i h j"),
+                in0=products[:, 0].rearrange("p i a (h j) -> p i (a h) j", h=2),
+                in1=products[:, 1].rearrange("p i a (h j) -> p i (a h) j", h=2),
+                op=ADD,
+            )
+
+        def store(projection, group, b, staged):
+            heads = outs[projection][b, group * TILES : (group + 1) * TILES]
+            nc.sync.dma_start(out=heads.rearrange("h (p i) j -> p h i j", i=TILES), in_=staged[:])
+
+        vstate = {"n": 0, "staged": None}
+        v_order = [(group, b, i) for group in range(2) for b in range(B) for i in range(TILES)]
+
+        def v_bank():
+            group, b, i = v_order[vstate["n"]]
+            vstate["n"] = vstate["n"] + 1
+            if i == 0:
+                vs = staged_pool.tile([P, TILES, TILES, HD], F32, name="staged")
+                vstate["staged"] = vs
+            plain = plain_psum.tile([P, ROWS], F32)
+            project(plain, b, i, (V, group))
+            nc.scalar.copy(out=vstate["staged"][:, :, i, :], in_=plain[:].rearrange("p (h j) -> p h j", h=TILES))
+            if i == TILES - 1:
+                store(V, group, b, vstate["staged"])
+
+        new_grouped(("x", 0))
+        new_grouped((Q, 0))
+        transpose_x(0, 0)
+        quantise(("x", 0), 0, 256)
+        for a in range(2):
+            transpose_w((Q, 0), a)
+            for g in range(PASSES):
+                quantise((Q, 0), (2 * g + a) * 256, 256)
+
+        units = [(projection, group, b) for group in range(2) for b in range(B) for projection in (Q, K)]
+        ahead = [(K, 0), ("x", 1), (V, 0), (Q, 1), (K, 1), (V, 1)]
+        v_banks = [0, 0, 0, 3, 3, 2, 4, 4]
+
+        for n, (projection, group, b) in enumerate(units):
+            if n > 0 and n < len(ahead):
+                key = ahead[n]
+                new_grouped(key)
+                for t in range(TILES):
+                    if key[0] == "x":
+                        transpose_x(1, t)
+                    elif t % 2 == 0:
+                        transpose_w(key, t // 2)
+            staged = staged_pool.tile([P, TILES, TILES, HD], F32)
+            v_left = v_banks[n]
+            for i in range(TILES):
+                acc = rotated_psum.tile([P, ROWS], F32)
+                project(acc, b, i, (projection, group))
+                if i % 2 == 0:
+                    products = product_pool.tile([P, 2, 2, 2, 2 * HD], F32)
+                multiply(acc, i, products, i % 2)
+                if n == 0 and i == 0:
+                    for t in range(1, TILES):
+                        transpose_x(0, t)
+                    quantise(("x", 0), 256, 256)
+                    quantise(("x", 0), 512, 512)
+                if n == 0 and i == 1:
+                    key = ahead[0]
+                    new_grouped(key)
+                    transpose_w(key, 0)
+                    transpose_w(key, 1)
+                if i % 2 == 1:
+                    add(products, staged, i - 1)
+                if i == (2 if n == 0 else 1) and n < len(ahead):
+                    for g in range(2):
+                        quantise(ahead[n], 512 * g, 512)
+                if v_left > 0 and n > 0:
+                    v_bank()
+                    v_left = v_left - 1
+            store(projection, group, b, staged)

@@ -236,8 +236,7 @@ def tile_attention_pa_kernel(tc, x, wq, wk, wv, freqs_cos, freqs_sin, out_0, out
                 if i % 2 == 1:
                     add(products, staged, i - 1)
                 if i == (2 if n == 0 else 1) and n < len(ahead):
-                    for g in range(2):
-                        quantise(ahead[n], 512 * g, 512)
+                    quantise(ahead[n], 0, 1024)
                 if v_left > 0 and n > 0:
                     v_bank()
                     v_left = v_left - 1

@@ -206,18 +206,25 @@ def tile_attention_pa_kernel(tc, x, wq, wk, wv, freqs_cos, freqs_sin, out_0, out
         ahead = [(K, 0), ("x", 1), (V, 0), (Q, 1), (K, 1), (V, 1)]
         v_banks = [0, 0, 0, 3, 3, 2, 4, 4]
 
+        def transpose_half(key, half):
+            if key[0] == "x":
+                transpose_x(key[1], 2 * half)
+                transpose_x(key[1], 2 * half + 1)
+            else:
+                transpose_w(key, half)
+
         for n, (projection, group, b) in enumerate(units):
-            if n > 0 and n < len(ahead):
-                key = ahead[n]
-                new_grouped(key)
-                for t in range(TILES):
-                    if key[0] == "x":
-                        transpose_x(1, t)
-                    elif t % 2 == 0:
-                        transpose_w(key, t // 2)
             staged = staged_pool.tile([P, TILES, TILES, HD], F32)
             v_left = v_banks[n]
             for i in range(TILES):
+                bank = n * TILES + i
+                for m, key in enumerate(ahead):
+                    first, second = (1, 2) if m == 0 else (4 * m - 1, 4 * m + 1)
+                    if bank == first:
+                        new_grouped(key)
+                        transpose_half(key, 0)
+                    if bank == second:
+                        transpose_half(key, 1)
                 acc = rotated_psum.tile([P, ROWS], F32)
                 project(acc, b, i, (projection, group))
                 if i % 2 == 0:
@@ -228,11 +235,6 @@ def tile_attention_pa_kernel(tc, x, wq, wk, wv, freqs_cos, freqs_sin, out_0, out
                         transpose_x(0, t)
                     quantise(("x", 0), 256, 256)
                     quantise(("x", 0), 512, 512)
-                if n == 0 and i == 1:
-                    key = ahead[0]
-                    new_grouped(key)
-                    transpose_w(key, 0)
-                    transpose_w(key, 1)
                 if i % 2 == 1:
                     add(products, staged, i - 1)
                 if i == (2 if n == 0 else 1) and n < len(ahead):

@@ -34,10 +34,11 @@ def tile_attention_pa_kernel(tc, x, wq, wk, wv, freqs_cos, freqs_sin, out_0, out
         ctx.enter_context(tc.manual_schedule())
         const = ctx.enter_context(tc.tile_pool(name="const", bufs=1))
         raw_pool = ctx.enter_context(tc.tile_pool(name="raw", bufs=8))
+        permuted_pool = ctx.enter_context(tc.tile_pool(name="permuted", bufs=2))
         grouped_pool = ctx.enter_context(tc.tile_pool(name="grouped", bufs=3))
         operand_pool = ctx.enter_context(tc.tile_pool(name="operand", bufs=8))
         product_pool = ctx.enter_context(tc.tile_pool(name="product", bufs=3))
-        staged_pool = ctx.enter_context(tc.tile_pool(name="staged", bufs=4))
+        staged_pool = ctx.enter_context(tc.tile_pool(name="staged", bufs=6))
         flipped_psum = ctx.enter_context(tc.psum_pool(name="flipped", bufs=3))
         rotated_psum = ctx.enter_context(tc.psum_pool(name="rotated", bufs=3))
         plain_psum = ctx.enter_context(tc.psum_pool(name="plain", bufs=2))
@@ -62,17 +63,18 @@ def tile_attention_pa_kernel(tc, x, wq, wk, wv, freqs_cos, freqs_sin, out_0, out
             for a in range(first, first + count):
                 nc.sync.dma_start(out=raws[(projection, group)][:, 2 * a : 2 * a + 2, :], in_=rows[a])
 
-        new_raw(("x", 0))
-        new_raw((Q, 0))
+        for key in [("x", 0), (Q, 0), ("x", 1), (K, 0), (V, 0), (Q, 1), (K, 1), (V, 1)]:
+            new_raw(key)
         load_x(0, 0, 1)
         load_w(Q, 0, 0, 2)
-        load_x(0, 1, 3)
-        for key in [(K, 0), ("x", 1), (V, 0), (Q, 1), (K, 1), (V, 1)]:
-            new_raw(key)
-            if key[0] == "x":
-                load_x(1, 0, 4)
-            else:
-                load_w(key[0], key[1], 0, 2)
+        load_x(0, 1, 1)
+        load_x(0, 2, 2)
+        load_x(1, 0, 4)
+        for key in [(K, 0), (V, 0), (Q, 1), (K, 1), (V, 1)]:
+            load_w(key[0], key[1], 0, 2)
+
+        zeros = const.tile([P, ROWS], BF16)
+        nc.vector.memset(zeros[:], 0.0)
 
         identity = const.tile([P, P], F32)
         make_identity(nc, identity[:])
@@ -93,13 +95,28 @@ def tile_attention_pa_kernel(tc, x, wq, wk, wv, freqs_cos, freqs_sin, out_0, out
         def words_of(key):
             return raws[key][:].rearrange("p t d -> p (t d)").bitcast(F32)
 
+        permuted = {}
+
+        def permute(key, t):
+            if t == 0:
+                words = permuted_pool.tile([P, TILES, PASSES, U, P], F32)
+                permuted[key] = words
+            nc.scalar.copy(
+                out=permuted[key][:, t],
+                in_=words_of(key)[:, t * 512 : (t + 1) * 512].rearrange("p (g r u) -> p g u r", g=2, u=U),
+            )
+
         def transpose4(key, picks):
             words = words_of(key)
             flipped = flipped_psum.tile([P, 2, U, P], F32)
             for j, (t, g) in enumerate(picks):
                 first = (t * PASSES + g) * 2 * P
                 for u in range(U):
-                    nc.tensor.transpose(flipped[:, j, u, :], words[:, first + u : first + 2 * P : 2], identity[:])
+                    if key in permuted:
+                        source = permuted[key][:, t, g, u, :]
+                    else:
+                        source = words[:, first + u : first + 2 * P : 2]
+                    nc.tensor.transpose(flipped[:, j, u, :], source, identity[:])
             return flipped
 
         def new_grouped(key):
@@ -166,17 +183,24 @@ def tile_attention_pa_kernel(tc, x, wq, wk, wv, freqs_cos, freqs_sin, out_0, out
                 op=MULT,
             )
 
-        def add(products, staged, first):
-            nc.gpsimd.tensor_tensor(
-                out=staged[:, :, first : first + 2, :].rearrange("p h i j -> p i h j"),
-                in0=products[:, 0].rearrange("p i a (h j) -> p i (a h) j", h=2),
-                in1=products[:, 1].rearrange("p i a (h j) -> p i (a h) j", h=2),
+        def add(engine, products, staged, first, count):
+            slot = first % 2
+            engine.tensor_tensor(
+                out=staged[:, :, first : first + count, :].rearrange("p h i j -> p i h j"),
+                in0=products[:, 0, slot : slot + count].rearrange("p i a (h j) -> p i (a h) j", h=2),
+                in1=products[:, 1, slot : slot + count].rearrange("p i a (h j) -> p i (a h) j", h=2),
                 op=ADD,
             )
 
-        def store(projection, group, b, staged):
+        def store(projection, group, b, staged, first=0, count=TILES):
             heads = outs[projection][b, group * TILES : (group + 1) * TILES]
-            nc.sync.dma_start(out=heads.rearrange("h (p i) j -> p h i j", i=TILES), in_=staged[:])
+            rows = heads.rearrange("h (p i) j -> p h i j", i=TILES)
+            nc.sync.dma_start(out=rows[:, :, first : first + count, :], in_=staged[:, :, first : first + count, :])
+
+        def warm(count):
+            idle = plain_psum.tile([P, ROWS], F32, name="plain")
+            for k in range(count):
+                nc.tensor.matmul(idle[:], zeros[:, 0:P], zeros[:], start=True, stop=True)
 
         vstate = {"n": 0, "staged": None}
         v_order = [(group, b, i) for group in range(2) for b in range(B) for i in range(TILES)]
@@ -187,7 +211,7 @@ def tile_attention_pa_kernel(tc, x, wq, wk, wv, freqs_cos, freqs_sin, out_0, out
             if i == 0:
                 vs = staged_pool.tile([P, TILES, TILES, HD], F32, name="staged")
                 vstate["staged"] = vs
-            plain = plain_psum.tile([P, ROWS], F32)
+            plain = plain_psum.tile([P, ROWS], F32, name="plain")
             project(plain, b, i, (V, group))
             nc.scalar.copy(out=vstate["staged"][:, :, i, :], in_=plain[:].rearrange("p (h j) -> p h j", h=TILES))
             if i == TILES - 1:
@@ -195,51 +219,56 @@ def tile_attention_pa_kernel(tc, x, wq, wk, wv, freqs_cos, freqs_sin, out_0, out
 
         new_grouped(("x", 0))
         new_grouped((Q, 0))
+        warm(4)
         transpose_x(0, 0)
         quantise(("x", 0), 0, 256)
+        warm(2)
         for a in range(2):
             transpose_w((Q, 0), a)
             for g in range(PASSES):
                 quantise((Q, 0), (2 * g + a) * 256, 256)
+            if a == 0:
+                warm(1)
+        transpose_x(0, 1)
+        quantise(("x", 0), 256, 256)
 
-        units = [(projection, group, b) for group in range(2) for b in range(B) for projection in (Q, K)]
-        ahead = [(K, 0), ("x", 1), (V, 0), (Q, 1), (K, 1), (V, 1)]
-        v_banks = [0, 0, 0, 3, 3, 2, 4, 4]
+        units = [(projection, group, b) for group in range(2) for projection in (Q, K) for b in range(B)]
+        ahead = [((K, 0), 3, 5), ((V, 0), 8, 9), ((Q, 1), 10, 12), ((K, 1), 15, 17), ((V, 1), 19, 20)]
+        v_after = [14 + n for n in range(8)] + [24 + n for n in range(8)]
 
-        def transpose_half(key, half):
-            if key[0] == "x":
-                transpose_x(key[1], 2 * half)
-                transpose_x(key[1], 2 * half + 1)
-            else:
-                transpose_w(key, half)
+        LAST = len(units) * TILES - 1
 
         for n, (projection, group, b) in enumerate(units):
             staged = staged_pool.tile([P, TILES, TILES, HD], F32)
-            v_left = v_banks[n]
             for i in range(TILES):
                 bank = n * TILES + i
-                for m, key in enumerate(ahead):
-                    first, second = (1, 2) if m == 0 else (4 * m - 1, 4 * m + 1)
+                for key, first, second in ahead:
+                    if key != (K, 0) and first - 4 <= bank < first:
+                        permute(key, bank - (first - 4))
                     if bank == first:
                         new_grouped(key)
-                        transpose_half(key, 0)
+                        transpose_w(key, 0)
                     if bank == second:
-                        transpose_half(key, 1)
+                        transpose_w(key, 1)
                 acc = rotated_psum.tile([P, ROWS], F32)
                 project(acc, b, i, (projection, group))
                 if i % 2 == 0:
                     products = product_pool.tile([P, 2, 2, 2, 2 * HD], F32)
                 multiply(acc, i, products, i % 2)
-                if n == 0 and i == 0:
-                    for t in range(1, TILES):
-                        transpose_x(0, t)
-                    quantise(("x", 0), 256, 256)
-                    quantise(("x", 0), 512, 512)
+                if bank < 6:
+                    tile = bank + 2
+                    if tile == TILES:
+                        new_grouped(("x", 1))
+                    transpose_x(tile // TILES, tile % TILES)
+                    quantise(("x", tile // TILES), 256 * (tile % TILES), 256)
                 if i % 2 == 1:
-                    add(products, staged, i - 1)
-                if i == (2 if n == 0 else 1) and n < len(ahead):
-                    quantise(ahead[n], 0, 1024)
-                if v_left > 0 and n > 0:
+                    add(nc.vector if bank == LAST else nc.gpsimd, products, staged, i - 1, 2)
+                    if n == len(units) - 1:
+                        store(projection, group, b, staged, i - 1, 2)
+                for key, first, second in ahead:
+                    if bank == second:
+                        quantise(key, 0, 1024)
+                for k in range(v_after.count(bank)):
                     v_bank()
-                    v_left = v_left - 1
-            store(projection, group, b, staged)
+            if n < len(units) - 1:
+                store(projection, group, b, staged)

@@ -33,11 +33,11 @@ def tile_attention_pa_kernel(tc, x, wq, wk, wv, freqs_cos, freqs_sin, out_0, out
     with ExitStack() as ctx:
         ctx.enter_context(tc.manual_schedule())
         const = ctx.enter_context(tc.tile_pool(name="const", bufs=1))
-        raw_pool = ctx.enter_context(tc.tile_pool(name="raw", bufs=8))
+        raw_pool = ctx.enter_context(tc.tile_pool(name="raw", bufs=6))
         permuted_pool = ctx.enter_context(tc.tile_pool(name="permuted", bufs=2))
         grouped_pool = ctx.enter_context(tc.tile_pool(name="grouped", bufs=3))
         operand_pool = ctx.enter_context(tc.tile_pool(name="operand", bufs=8))
-        product_pool = ctx.enter_context(tc.tile_pool(name="product", bufs=3))
+        product_pool = ctx.enter_context(tc.tile_pool(name="product", bufs=2))
         staged_pool = ctx.enter_context(tc.tile_pool(name="staged", bufs=6))
         flipped_psum = ctx.enter_context(tc.psum_pool(name="flipped", bufs=3))
         rotated_psum = ctx.enter_context(tc.psum_pool(name="rotated", bufs=3))
@@ -63,14 +63,16 @@ def tile_attention_pa_kernel(tc, x, wq, wk, wv, freqs_cos, freqs_sin, out_0, out
             for a in range(first, first + count):
                 nc.sync.dma_start(out=raws[(projection, group)][:, 2 * a : 2 * a + 2, :], in_=rows[a])
 
-        for key in [("x", 0), (Q, 0), ("x", 1), (K, 0), (V, 0), (Q, 1), (K, 1), (V, 1)]:
+        for key in [("x", 0), (Q, 0), ("x", 1)]:
             new_raw(key)
         load_x(0, 0, 1)
         load_w(Q, 0, 0, 2)
         load_x(0, 1, 1)
         load_x(0, 2, 2)
         load_x(1, 0, 4)
-        for key in [(K, 0), (V, 0), (Q, 1), (K, 1), (V, 1)]:
+        later = [(K, 0), (V, 0), (Q, 1), (V, 1), (K, 1)]
+        for key in later:
+            new_raw(key)
             load_w(key[0], key[1], 0, 2)
 
         zeros = const.tile([P, ROWS], BF16)
@@ -159,11 +161,11 @@ def tile_attention_pa_kernel(tc, x, wq, wk, wv, freqs_cos, freqs_sin, out_0, out
                 in_=grouped[key][:, first * PACK : (first + count) * PACK],
             )
 
-        def project(acc, b, i, key):
+        def project(acc, b, i, key, first=0, count=ROWS):
             xk = ("x", b)
             for g in range(PASSES):
                 tokens = slice((i * PASSES + g) * P, (i * PASSES + g + 1) * P)
-                rows = slice(g * ROWS, (g + 1) * ROWS)
+                rows = slice(g * ROWS + first, g * ROWS + first + count)
                 nc.tensor.matmul_mx(
                     out=acc[:],
                     lhsT=codes[xk][:, tokens].bitcast(FP8X4),
@@ -184,7 +186,7 @@ def tile_attention_pa_kernel(tc, x, wq, wk, wv, freqs_cos, freqs_sin, out_0, out
             )
 
         def add(engine, products, staged, first, count):
-            slot = first % 2
+            slot = first
             engine.tensor_tensor(
                 out=staged[:, :, first : first + count, :].rearrange("p h i j -> p i h j"),
                 in0=products[:, 0, slot : slot + count].rearrange("p i a (h j) -> p i (a h) j", h=2),
@@ -217,6 +219,9 @@ def tile_attention_pa_kernel(tc, x, wq, wk, wv, freqs_cos, freqs_sin, out_0, out
             if i == TILES - 1:
                 store(V, group, b, vstate["staged"])
 
+        units = [(p, g, b) for g in range(2) for p in (Q, K) for b in range(B)]
+        ahead = [(key, 4 * m + 3 if m else 4, 4 * m + 5) for m, key in enumerate(later)]
+
         new_grouped(("x", 0))
         new_grouped((Q, 0))
         warm(4)
@@ -227,23 +232,18 @@ def tile_attention_pa_kernel(tc, x, wq, wk, wv, freqs_cos, freqs_sin, out_0, out
             transpose_w((Q, 0), a)
             for g in range(PASSES):
                 quantise((Q, 0), (2 * g + a) * 256, 256)
-            if a == 0:
-                warm(1)
         transpose_x(0, 1)
         quantise(("x", 0), 256, 256)
-
-        units = [(projection, group, b) for group in range(2) for projection in (Q, K) for b in range(B)]
-        ahead = [((K, 0), 3, 5), ((V, 0), 8, 9), ((Q, 1), 10, 12), ((K, 1), 15, 17), ((V, 1), 19, 20)]
-        v_after = [14 + n for n in range(8)] + [24 + n for n in range(8)]
 
         LAST = len(units) * TILES - 1
 
         for n, (projection, group, b) in enumerate(units):
             staged = staged_pool.tile([P, TILES, TILES, HD], F32)
+            products = product_pool.tile([P, 2, TILES, 2, 2 * HD], F32)
             for i in range(TILES):
                 bank = n * TILES + i
                 for key, first, second in ahead:
-                    if key != (K, 0) and first - 4 <= bank < first:
+                    if key[1] == 1 and first - 4 <= bank < first:
                         permute(key, bank - (first - 4))
                     if bank == first:
                         new_grouped(key)
@@ -252,23 +252,24 @@ def tile_attention_pa_kernel(tc, x, wq, wk, wv, freqs_cos, freqs_sin, out_0, out
                         transpose_w(key, 1)
                 acc = rotated_psum.tile([P, ROWS], F32)
                 project(acc, b, i, (projection, group))
-                if i % 2 == 0:
-                    products = product_pool.tile([P, 2, 2, 2, 2 * HD], F32)
-                multiply(acc, i, products, i % 2)
-                if bank < 6:
-                    tile = bank + 2
-                    if tile == TILES:
-                        new_grouped(("x", 1))
-                    transpose_x(tile // TILES, tile % TILES)
-                    quantise(("x", tile // TILES), 256 * (tile % TILES), 256)
-                if i % 2 == 1:
+                multiply(acc, i, products, i)
+                if bank < 3:
+                    half_b, half = divmod(bank + 1, 2)
+                    if half == 0:
+                        new_grouped(("x", half_b))
+                    for t in range(2):
+                        transpose_x(half_b, 2 * half + t)
+                    quantise(("x", half_b), 512 * half, 512)
+                if bank < 2:
+                    add(nc.gpsimd if i else nc.vector, products, staged, i, 1)
+                elif i % 2 == 1:
                     add(nc.vector if bank == LAST else nc.gpsimd, products, staged, i - 1, 2)
                     if n == len(units) - 1:
                         store(projection, group, b, staged, i - 1, 2)
                 for key, first, second in ahead:
                     if bank == second:
                         quantise(key, 0, 1024)
-                for k in range(v_after.count(bank)):
+                if 12 <= bank < 28:
                     v_bank()
             if n < len(units) - 1:
                 store(projection, group, b, staged)

@@ -177,20 +177,18 @@ def tile_attention_pa_kernel(tc, x, wq, wk, wv, freqs_cos, freqs_sin, out_0, out
                 )
 
         def multiply(acc, i, products, slot):
-            shape = [P, 2, 2 * P, 2]
             nc.vector.tensor_tensor(
-                out=products[:, :, slot, :, :].rearrange("p e a (q d) -> p a e q d", d=2),
+                out=products[:, slot].rearrange("p e a (q d) -> p a e q d", d=2),
                 in0=acc[:].rearrange("p (a e q) -> p a e q", a=2, e=2).unsqueeze(4).to_broadcast([P, 2, 2, P, 2]),
                 in1=factors[:, i].rearrange("p e h (n d) -> p e (h n) d", d=2).unsqueeze(1).to_broadcast([P, 2, 2, P, 2]),
                 op=MULT,
             )
 
         def add(engine, products, staged, first, count):
-            slot = first
             engine.tensor_tensor(
                 out=staged[:, :, first : first + count, :].rearrange("p h i j -> p i h j"),
-                in0=products[:, 0, slot : slot + count].rearrange("p i a (h j) -> p i (a h) j", h=2),
-                in1=products[:, 1, slot : slot + count].rearrange("p i a (h j) -> p i (a h) j", h=2),
+                in0=products[:, first : first + count, 0].rearrange("p i a (h j) -> p i (a h) j", h=2),
+                in1=products[:, first : first + count, 1].rearrange("p i a (h j) -> p i (a h) j", h=2),
                 op=ADD,
             )
 
@@ -239,7 +237,7 @@ def tile_attention_pa_kernel(tc, x, wq, wk, wv, freqs_cos, freqs_sin, out_0, out
 
         for n, (projection, group, b) in enumerate(units):
             staged = staged_pool.tile([P, TILES, TILES, HD], F32)
-            products = product_pool.tile([P, 2, TILES, 2, 2 * HD], F32)
+            products = product_pool.tile([P, TILES, 2, 2, 2 * HD], F32)
             for i in range(TILES):
                 bank = n * TILES + i
                 for key, first, second in ahead:

@@ -232,6 +232,7 @@ def tile_attention_pa_kernel(tc, x, wq, wk, wv, freqs_cos, freqs_sin, out_0, out
                 quantise((Q, 0), (2 * g + a) * 256, 256)
         transpose_x(0, 1)
         quantise(("x", 0), 256, 256)
+        warm(1)
 
         LAST = len(units) * TILES - 1
 
@@ -243,6 +244,9 @@ def tile_attention_pa_kernel(tc, x, wq, wk, wv, freqs_cos, freqs_sin, out_0, out
                 for key, first, second in ahead:
                     if key[1] == 1 and first - 4 <= bank < first:
                         permute(key, bank - (first - 4))
+                    if key == (K, 0) and first - 2 <= bank < first:
+                        permute(key, 2 * (bank - (first - 2)))
+                        permute(key, 2 * (bank - (first - 2)) + 1)
                     if bank == first:
                         new_grouped(key)
                         transpose_w(key, 0)

@@ -39,13 +39,14 @@ def tile_attention_pa_kernel(tc, x, wq, wk, wv, freqs_cos, freqs_sin, out_0, out
         operand_pool = ctx.enter_context(tc.tile_pool(name="operand", bufs=8))
         product_pool = ctx.enter_context(tc.tile_pool(name="product", bufs=2))
         staged_pool = ctx.enter_context(tc.tile_pool(name="staged", bufs=6))
+        half_pool = ctx.enter_context(tc.tile_pool(name="half", bufs=2))
         flipped_psum = ctx.enter_context(tc.psum_pool(name="flipped", bufs=3))
         rotated_psum = ctx.enter_context(tc.psum_pool(name="rotated", bufs=3))
         plain_psum = ctx.enter_context(tc.psum_pool(name="plain", bufs=2))
 
         tables = const.tile([P, 3, TILES * PAIRS], BF16)
-        nc.scalar.dma_start(out=tables[:, 1, :], in_=freqs_cos.rearrange("(p i) n -> p (i n)", i=TILES))
-        nc.scalar.dma_start(out=tables[:, 2, :], in_=freqs_sin.rearrange("(p i) n -> p (i n)", i=TILES))
+        nc.scalar.dma_start(out=tables[:, 0, :], in_=freqs_cos.rearrange("(p i) n -> p (i n)", i=TILES))
+        nc.scalar.dma_start(out=tables[:, 1, :], in_=freqs_sin.rearrange("(p i) n -> p (i n)", i=TILES))
 
         raws = {}
 
@@ -81,14 +82,17 @@ def tile_attention_pa_kernel(tc, x, wq, wk, wv, freqs_cos, freqs_sin, out_0, out
         identity = const.tile([P, P], F32)
         make_identity(nc, identity[:])
 
-        factors = const.tile([P, TILES, 2, 2, HD], BF16)
-        nc.vector.tensor_scalar_mul(out=tables[:, 0, :], in0=tables[:, 2, :], scalar1=-1.0)
-        for e in range(2):
-            for h in range(2):
-                nc.vector.tensor_copy(
-                    out=factors[:, :, e, h, :].rearrange("p i (n d) -> p i n d", d=2),
-                    in_=tables[:, 1 - e : 3 - e, :].rearrange("p d (i n) -> p i n d", i=TILES),
-                )
+        factors = const.tile([P, TILES, 2, HD], BF16)
+        nc.vector.tensor_scalar_mul(out=tables[:, 2, :], in0=tables[:, 1, :], scalar1=-1.0)
+        pairs = [P, TILES, PAIRS, 2]
+        nc.vector.tensor_copy(
+            out=factors[:, :, 0, :].rearrange("p i (n d) -> p i n d", d=2),
+            in_=tables[:, 0, :].rearrange("p (i n) -> p i n", i=TILES).unsqueeze(3).to_broadcast(pairs),
+        )
+        nc.vector.tensor_copy(
+            out=factors[:, :, 1, :].rearrange("p i (n d) -> p i n d", d=2),
+            in_=tables[:, 1:3, :].rearrange("p d (i n) -> p i n d", i=TILES),
+        )
 
         grouped = {}
         codes = {}
@@ -143,16 +147,10 @@ def tile_attention_pa_kernel(tc, x, wq, wk, wv, freqs_cos, freqs_sin, out_0, out
             for g in range(PASSES):
                 flipped = transpose4(key, [(2 * a, g), (2 * a + 1, g)])
                 out = words[:, (2 * g + a) * 512 : (2 * g + a + 1) * 512]
-                if key[0] == V:
-                    nc.scalar.copy(
-                        out=out.rearrange("p (r e u) -> p r e u", e=2, u=U),
-                        in_=flipped[:].rearrange("p e u r -> p r e u"),
-                    )
-                else:
-                    nc.scalar.copy(
-                        out=out.rearrange("p (e r u) -> p e r u", e=2, u=U),
-                        in_=flipped[:].rearrange("p e u r -> p e r u"),
-                    )
+                nc.scalar.copy(
+                    out=out.rearrange("p (r e u) -> p r e u", e=2, u=U),
+                    in_=flipped[:].rearrange("p e u r -> p r e u"),
+                )
 
         def quantise(key, first, count):
             nc.vector.quantize_mx(
@@ -177,25 +175,27 @@ def tile_attention_pa_kernel(tc, x, wq, wk, wv, freqs_cos, freqs_sin, out_0, out
                 )
 
         def multiply(acc, i, products, slot):
+            shape = [P, 2, TILES, HD]
             nc.vector.tensor_tensor(
-                out=products[:, slot].rearrange("p e a (q d) -> p a e q d", d=2),
-                in0=acc[:].rearrange("p (a e q) -> p a e q", a=2, e=2).unsqueeze(4).to_broadcast([P, 2, 2, P, 2]),
-                in1=factors[:, i].rearrange("p e h (n d) -> p e (h n) d", d=2).unsqueeze(1).to_broadcast([P, 2, 2, P, 2]),
+                out=products[:, slot].rearrange("p k (h j) -> p k h j", h=TILES),
+                in0=acc[:].rearrange("p (h j) -> p h j", h=TILES).unsqueeze(1).to_broadcast(shape),
+                in1=factors[:, i].unsqueeze(2).to_broadcast(shape),
                 op=MULT,
             )
 
-        def add(engine, products, staged, first, count):
+        def add(engine, products, first, count, sums):
+            slots = products[:, first : first + count].rearrange("p i k (h n d) -> p k i h n d", h=TILES, d=2)
             engine.tensor_tensor(
-                out=staged[:, :, first : first + count, :].rearrange("p h i j -> p i h j"),
-                in0=products[:, first : first + count, 0].rearrange("p i a (h j) -> p i (a h) j", h=2),
-                in1=products[:, first : first + count, 1].rearrange("p i a (h j) -> p i (a h) j", h=2),
+                out=sums.rearrange("p h i (n d) -> p i h n d", d=2),
+                in0=slots[:, 0],
+                in1=slots[:, 1][:, :, :, :, ::-1],
                 op=ADD,
             )
 
         def store(projection, group, b, staged, first=0, count=TILES):
             heads = outs[projection][b, group * TILES : (group + 1) * TILES]
             rows = heads.rearrange("h (p i) j -> p h i j", i=TILES)
-            nc.sync.dma_start(out=rows[:, :, first : first + count, :], in_=staged[:, :, first : first + count, :])
+            nc.sync.dma_start(out=rows[:, :, first : first + count, :], in_=staged[:])
 
         def warm(count):
             idle = plain_psum.tile([P, ROWS], F32, name="plain")
@@ -237,8 +237,10 @@ def tile_attention_pa_kernel(tc, x, wq, wk, wv, freqs_cos, freqs_sin, out_0, out
         LAST = len(units) * TILES - 1
 
         for n, (projection, group, b) in enumerate(units):
-            staged = staged_pool.tile([P, TILES, TILES, HD], F32)
-            products = product_pool.tile([P, TILES, 2, 2, 2 * HD], F32)
+            last_unit = n == len(units) - 1
+            if not last_unit:
+                staged = staged_pool.tile([P, TILES, TILES, HD], F32, name="staged")
+            products = product_pool.tile([P, TILES, 2, ROWS], F32)
             for i in range(TILES):
                 bank = n * TILES + i
                 for key, first, second in ahead:
@@ -263,15 +265,20 @@ def tile_attention_pa_kernel(tc, x, wq, wk, wv, freqs_cos, freqs_sin, out_0, out
                         transpose_x(half_b, 2 * half + t)
                     quantise(("x", half_b), 512 * half, 512)
                 if bank < 2:
-                    add(nc.gpsimd if i else nc.vector, products, staged, i, 1)
+                    add(nc.gpsimd if i else nc.vector, products, i, 1, staged[:, :, i : i + 1, :])
                 elif i % 2 == 1:
-                    add(nc.vector if bank == LAST else nc.gpsimd, products, staged, i - 1, 2)
-                    if n == len(units) - 1:
-                        store(projection, group, b, staged, i - 1, 2)
+                    if last_unit:
+                        half = half_pool.tile([P, TILES, 2, HD], F32)
+                        sums = half[:]
+                    else:
+                        sums = staged[:, :, i - 1 : i + 1, :]
+                    add(nc.vector if bank == LAST else nc.gpsimd, products, i - 1, 2, sums)
+                    if last_unit:
+                        store(projection, group, b, half, i - 1, 2)
                 for key, first, second in ahead:
                     if bank == second:
                         quantise(key, 0, 1024)
                 if 12 <= bank < 28:
                     v_bank()
-            if n < len(units) - 1:
+            if not last_unit:
                 store(projection, group, b, staged)

@@ -38,8 +38,8 @@ def tile_attention_pa_kernel(tc, x, wq, wk, wv, freqs_cos, freqs_sin, out_0, out
         grouped_pool = ctx.enter_context(tc.tile_pool(name="grouped", bufs=3))
         operand_pool = ctx.enter_context(tc.tile_pool(name="operand", bufs=8))
         product_pool = ctx.enter_context(tc.tile_pool(name="product", bufs=2))
-        staged_pool = ctx.enter_context(tc.tile_pool(name="staged", bufs=6))
-        half_pool = ctx.enter_context(tc.tile_pool(name="half", bufs=2))
+        staged_pool = ctx.enter_context(tc.tile_pool(name="staged", bufs=3))
+        sums_pool = ctx.enter_context(tc.tile_pool(name="sums", bufs=8))
         flipped_psum = ctx.enter_context(tc.psum_pool(name="flipped", bufs=3))
         rotated_psum = ctx.enter_context(tc.psum_pool(name="rotated", bufs=3))
         plain_psum = ctx.enter_context(tc.psum_pool(name="plain", bufs=2))
@@ -192,10 +192,10 @@ def tile_attention_pa_kernel(tc, x, wq, wk, wv, freqs_cos, freqs_sin, out_0, out
                 op=ADD,
             )
 
-        def store(projection, group, b, staged, first=0, count=TILES):
+        def store(projection, group, b, staged, first, count, queue):
             heads = outs[projection][b, group * TILES : (group + 1) * TILES]
             rows = heads.rearrange("h (p i) j -> p h i j", i=TILES)
-            nc.sync.dma_start(out=rows[:, :, first : first + count, :], in_=staged[:])
+            queue.dma_start(out=rows[:, :, first : first + count, :], in_=staged[:])
 
         def warm(count):
             idle = plain_psum.tile([P, ROWS], F32, name="plain")
@@ -215,7 +215,7 @@ def tile_attention_pa_kernel(tc, x, wq, wk, wv, freqs_cos, freqs_sin, out_0, out
             project(plain, b, i, (V, group))
             nc.scalar.copy(out=vstate["staged"][:, :, i, :], in_=plain[:].rearrange("p (h j) -> p h j", h=TILES))
             if i == TILES - 1:
-                store(V, group, b, vstate["staged"])
+                store(V, group, b, vstate["staged"], 0, TILES, nc.scalar)
 
         units = [(p, g, b) for g in range(2) for p in (Q, K) for b in range(B)]
         ahead = [(key, 4 * m + 3 if m else 4, 4 * m + 5) for m, key in enumerate(later)]
@@ -237,9 +237,6 @@ def tile_attention_pa_kernel(tc, x, wq, wk, wv, freqs_cos, freqs_sin, out_0, out
         LAST = len(units) * TILES - 1
 
         for n, (projection, group, b) in enumerate(units):
-            last_unit = n == len(units) - 1
-            if not last_unit:
-                staged = staged_pool.tile([P, TILES, TILES, HD], F32, name="staged")
             products = product_pool.tile([P, TILES, 2, ROWS], F32)
             for i in range(TILES):
                 bank = n * TILES + i
@@ -264,21 +261,16 @@ def tile_attention_pa_kernel(tc, x, wq, wk, wv, freqs_cos, freqs_sin, out_0, out
                     for t in range(2):
                         transpose_x(half_b, 2 * half + t)
                     quantise(("x", half_b), 512 * half, 512)
+                if i % 2 == 0:
+                    sums = sums_pool.tile([P, TILES, 2, HD], F32)
                 if bank < 2:
-                    add(nc.gpsimd if i else nc.vector, products, i, 1, staged[:, :, i : i + 1, :])
+                    add(nc.gpsimd if i else nc.vector, products, i, 1, sums[:, :, i : i + 1, :])
                 elif i % 2 == 1:
-                    if last_unit:
-                        half = half_pool.tile([P, TILES, 2, HD], F32)
-                        sums = half[:]
-                    else:
-                        sums = staged[:, :, i - 1 : i + 1, :]
-                    add(nc.vector if bank == LAST else nc.gpsimd, products, i - 1, 2, sums)
-                    if last_unit:
-                        store(projection, group, b, half, i - 1, 2)
+                    add(nc.vector if bank == LAST else nc.gpsimd, products, i - 1, 2, sums[:])
+                if i % 2 == 1:
+                    store(projection, group, b, sums, i - 1, 2, nc.sync)
                 for key, first, second in ahead:
                     if bank == second:
                         quantise(key, 0, 1024)
                 if 12 <= bank < 28:
                     v_bank()
-            if not last_unit:
-                store(projection, group, b, staged)

from contextlib import ExitStack

import concourse.mybir as mybir
from concourse.masks import make_identity

F32 = mybir.dt.float32
BF16 = mybir.dt.bfloat16
U32 = mybir.dt.uint32
U8 = mybir.dt.uint8
FP8X4 = mybir.dt.float8_e4m3fn_x4
MULT = mybir.AluOpType.mult
ADD = mybir.AluOpType.add

B, S, D, H, HD = 2, 512, 1024, 8, 128
P = 128
PACK = 4
K_PASS = P * PACK
PASSES = D // K_PASS
U = 2
TILES = 4
ROWS = TILES * P
PAIRS = HD // 2
Q, K, V = 0, 1, 2

FLOPS = 2 * B * S * D * 3 * H * HD


def tile_attention_pa_kernel(tc, x, wq, wk, wv, freqs_cos, freqs_sin, out_0, out_1, out_2):
    nc = tc.nc
    weights = [wq, wk, wv]
    outs = [out_0, out_1, out_2]

    with ExitStack() as ctx:
        ctx.enter_context(tc.manual_schedule())
        const = ctx.enter_context(tc.tile_pool(name="const", bufs=1))
        raw_pool = ctx.enter_context(tc.tile_pool(name="raw", bufs=6))
        permuted_pool = ctx.enter_context(tc.tile_pool(name="permuted", bufs=2))
        grouped_pool = ctx.enter_context(tc.tile_pool(name="grouped", bufs=3))
        operand_pool = ctx.enter_context(tc.tile_pool(name="operand", bufs=8))
        product_pool = ctx.enter_context(tc.tile_pool(name="product", bufs=2))
        staged_pool = ctx.enter_context(tc.tile_pool(name="staged", bufs=3))
        sums_pool = ctx.enter_context(tc.tile_pool(name="sums", bufs=8))
        flipped_psum = ctx.enter_context(tc.psum_pool(name="flipped", bufs=3))
        rotated_psum = ctx.enter_context(tc.psum_pool(name="rotated", bufs=3))
        plain_psum = ctx.enter_context(tc.psum_pool(name="plain", bufs=2))

        tables = const.tile([P, 3, TILES * PAIRS], BF16)
        nc.scalar.dma_start(out=tables[:, 0, :], in_=freqs_cos.rearrange("(p i) n -> p (i n)", i=TILES))
        nc.scalar.dma_start(out=tables[:, 1, :], in_=freqs_sin.rearrange("(p i) n -> p (i n)", i=TILES))

        raws = {}

        def new_raw(key):
            raw = raw_pool.tile([P, TILES, D], BF16)
            raws[key] = raw

        def load_x(b, first, count):
            rows = x[b].rearrange("(p i) d -> p i d", i=TILES)
            nc.sync.dma_start(out=raws[("x", b)][:, first : first + count, :], in_=rows[:, first : first + count, :])

        def load_w(projection, group, first, count):
            heads = weights[projection][group * TILES : (group + 1) * TILES]
            rows = heads.rearrange("(a h) (n e) d -> a (h n) e d", a=2, e=2)
            for a in range(first, first + count):
                nc.sync.dma_start(out=raws[(projection, group)][:, 2 * a : 2 * a + 2, :], in_=rows[a])

        for key in [("x", 0), (Q, 0), ("x", 1)]:
            new_raw(key)
        load_x(0, 0, 1)
        load_w(Q, 0, 0, 2)
        load_x(0, 1, 1)
        load_x(0, 2, 2)
        load_x(1, 0, 4)
        later = [(K, 0), (V, 0), (Q, 1), (V, 1), (K, 1)]
        for key in later:
            new_raw(key)
            load_w(key[0], key[1], 0, 2)

        zeros = const.tile([P, ROWS], BF16)
        nc.vector.memset(zeros[:], 0.0)

        identity = const.tile([P, P], F32)
        make_identity(nc, identity[:])

        factors = const.tile([P, TILES, 2, HD], BF16)
        nc.vector.tensor_scalar_mul(out=tables[:, 2, :], in0=tables[:, 1, :], scalar1=-1.0)
        pairs = [P, TILES, PAIRS, 2]
        nc.vector.tensor_copy(
            out=factors[:, :, 0, :].rearrange("p i (n d) -> p i n d", d=2),
            in_=tables[:, 0, :].rearrange("p (i n) -> p i n", i=TILES).unsqueeze(3).to_broadcast(pairs),
        )
        nc.vector.tensor_copy(
            out=factors[:, :, 1, :].rearrange("p i (n d) -> p i n d", d=2),
            in_=tables[:, 1:3, :].rearrange("p d (i n) -> p i n d", i=TILES),
        )

        grouped = {}
        codes = {}
        scales = {}

        def words_of(key):
            return raws[key][:].rearrange("p t d -> p (t d)").bitcast(F32)

        permuted = {}

        def permute(key, t):
            if t == 0:
                words = permuted_pool.tile([P, TILES, PASSES, U, P], F32)
                permuted[key] = words
            nc.scalar.copy(
                out=permuted[key][:, t],
                in_=words_of(key)[:, t * 512 : (t + 1) * 512].rearrange("p (g r u) -> p g u r", g=2, u=U),
            )

        def transpose4(key, picks):
            words = words_of(key)
            flipped = flipped_psum.tile([P, 2, U, P], F32)
            for j, (t, g) in enumerate(picks):
                first = (t * PASSES + g) * 2 * P
                for u in range(U):
                    if key in permuted:
                        source = permuted[key][:, t, g, u, :]
                    else:
                        source = words[:, first + u : first + 2 * P : 2]
                    nc.tensor.transpose(flipped[:, j, u, :], source, identity[:])
            return flipped

        def new_grouped(key):
            g = grouped_pool.tile([P, 2 * ROWS * PACK], BF16, align_bytes=64)
            grouped[key] = g
            c = operand_pool.tile([P, 2 * ROWS], U32, align_bytes=64)
            s = operand_pool.tile([P, 2 * ROWS], U8, align_bytes=64)
            codes[key] = c
            scales[key] = s

        def transpose_x(b, t):
            key = ("x", b)
            flipped = transpose4(key, [(t, 0), (t, 1)])
            words = grouped[key][:].bitcast(F32)
            nc.scalar.copy(
                out=words[:, t * 512 : (t + 1) * 512].rearrange("p (g r u) -> p g r u", g=2, u=U),
                in_=flipped[:].rearrange("p g u r -> p g r u"),
            )

        def transpose_w(key, a):
            words = grouped[key][:].bitcast(F32)
            for g in range(PASSES):
                flipped = transpose4(key, [(2 * a, g), (2 * a + 1, g)])
                out = words[:, (2 * g + a) * 512 : (2 * g + a + 1) * 512]
                nc.scalar.copy(
                    out=out.rearrange("p (r e u) -> p r e u", e=2, u=U),
                    in_=flipped[:].rearrange("p e u r -> p r e u"),
                )

        def quantise(key, first, count):
            nc.vector.quantize_mx(
                out=codes[key][:, first : first + count].bitcast(FP8X4),
                scales=scales[key][:, first : first + count],
                in_=grouped[key][:, first * PACK : (first + count) * PACK],
            )

        def project(acc, b, i, key, first=0, count=ROWS):
            xk = ("x", b)
            for g in range(PASSES):
                tokens = slice((i * PASSES + g) * P, (i * PASSES + g + 1) * P)
                rows = slice(g * ROWS + first, g * ROWS + first + count)
                nc.tensor.matmul_mx(
                    out=acc[:],
                    lhsT=codes[xk][:, tokens].bitcast(FP8X4),
                    lhsT_scale=scales[xk][:, tokens],
                    rhs=codes[key][:, rows].bitcast(FP8X4),
                    rhs_scale=scales[key][:, rows],
                    start=(g == 0),
                    stop=(g == PASSES - 1),
                )

        def multiply(acc, i, products, slot):
            shape = [P, 2, TILES, HD]
            nc.vector.tensor_tensor(
                out=products[:, slot].rearrange("p k (h j) -> p k h j", h=TILES),
                in0=acc[:].rearrange("p (h j) -> p h j", h=TILES).unsqueeze(1).to_broadcast(shape),
                in1=factors[:, i].unsqueeze(2).to_broadcast(shape),
                op=MULT,
            )

        def add(engine, products, first, count, sums):
            slots = products[:, first : first + count].rearrange("p i k (h n d) -> p k i h n d", h=TILES, d=2)
            engine.tensor_tensor(
                out=sums.rearrange("p h i (n d) -> p i h n d", d=2),
                in0=slots[:, 0],
                in1=slots[:, 1][:, :, :, :, ::-1],
                op=ADD,
            )

        def store(projection, group, b, staged, first, count, queue):
            heads = outs[projection][b, group * TILES : (group + 1) * TILES]
            rows = heads.rearrange("h (p i) j -> p h i j", i=TILES)
            queue.dma_start(out=rows[:, :, first : first + count, :], in_=staged[:])

        def warm(count):
            idle = plain_psum.tile([P, ROWS], F32, name="plain")
            for k in range(count):
                nc.tensor.matmul(idle[:], zeros[:, 0:P], zeros[:], start=True, stop=True)

        vstate = {"n": 0, "staged": None}
        v_order = [(group, b, i) for group in range(2) for b in range(B) for i in range(TILES)]

        def v_bank():
            group, b, i = v_order[vstate["n"]]
            vstate["n"] = vstate["n"] + 1
            if i == 0:
                vs = staged_pool.tile([P, TILES, TILES, HD], F32, name="staged")
                vstate["staged"] = vs
            plain = plain_psum.tile([P, ROWS], F32, name="plain")
            project(plain, b, i, (V, group))
            nc.scalar.copy(out=vstate["staged"][:, :, i, :], in_=plain[:].rearrange("p (h j) -> p h j", h=TILES))
            if i == TILES - 1:
                store(V, group, b, vstate["staged"], 0, TILES, nc.scalar)

        units = [(p, g, b) for g in range(2) for p in (Q, K) for b in range(B)]
        ahead = [(key, 4 * m + 3 if m else 4, 4 * m + 5) for m, key in enumerate(later)]

        new_grouped(("x", 0))
        new_grouped((Q, 0))
        warm(4)
        transpose_x(0, 0)
        quantise(("x", 0), 0, 256)
        warm(2)
        for a in range(2):
            transpose_w((Q, 0), a)
            for g in range(PASSES):
                quantise((Q, 0), (2 * g + a) * 256, 256)
        transpose_x(0, 1)
        quantise(("x", 0), 256, 256)
        warm(1)

        LAST = len(units) * TILES - 1

        for n, (projection, group, b) in enumerate(units):
            products = product_pool.tile([P, TILES, 2, ROWS], F32)
            for i in range(TILES):
                bank = n * TILES + i
                for key, first, second in ahead:
                    if key[1] == 1 and first - 4 <= bank < first:
                        permute(key, bank - (first - 4))
                    if key == (K, 0) and first - 2 <= bank < first:
                        permute(key, 2 * (bank - (first - 2)))
                        permute(key, 2 * (bank - (first - 2)) + 1)
                    if bank == first:
                        new_grouped(key)
                        transpose_w(key, 0)
                    if bank == second:
                        transpose_w(key, 1)
                acc = rotated_psum.tile([P, ROWS], F32)
                project(acc, b, i, (projection, group))
                multiply(acc, i, products, i)
                if bank < 3:
                    half_b, half = divmod(bank + 1, 2)
                    if half == 0:
                        new_grouped(("x", half_b))
                    for t in range(2):
                        transpose_x(half_b, 2 * half + t)
                    quantise(("x", half_b), 512 * half, 512)
                if i % 2 == 0:
                    sums = sums_pool.tile([P, TILES, 2, HD], F32)
                if bank < 2:
                    add(nc.gpsimd if i else nc.vector, products, i, 1, sums[:, :, i : i + 1, :])
                elif i % 2 == 1:
                    add(nc.vector if bank == LAST else nc.gpsimd, products, i - 1, 2, sums[:])
                if i % 2 == 1:
                    store(projection, group, b, sums, i - 1, 2, nc.sync)
                for key, first, second in ahead:
                    if bank == second:
                        quantise(key, 0, 1024)
                if 12 <= bank < 28:
                    v_bank()
